import numpy as np
import ml_dtypes


def mxq(x, axis, fmt="e4m3"):
    dtype, down = {"e4m3": (ml_dtypes.float8_e4m3fn, 7), "e5m2": (ml_dtypes.float8_e5m2, 14)}[fmt]
    v = np.moveaxis(np.asarray(x, np.float32).astype(ml_dtypes.bfloat16).astype(np.float64), axis, -1)
    blocks = v.reshape(v.shape[:-1] + (-1, 32))
    amax = np.abs(blocks).max(-1, keepdims=True)
    byte = np.maximum(np.where(amax > 0, np.frexp(amax)[1] - 1 + 127, 0) - down, 1)
    scale = np.exp2(byte - 127.0)
    codes = (blocks / scale).astype(np.float32).astype(dtype).astype(np.float64)
    return np.moveaxis((codes * scale).reshape(v.shape), -1, axis)


WIDE = False


def mx_kscale(k):
    if not WIDE:
        return np.ones(k)
    levels = np.array([10, -10, 5, -5, 0])
    if k % 512:
        return np.exp2(np.random.permutation(np.resize(levels, k // 32))).repeat(32)
    a = np.empty((k // 512, 16))
    for p in range(k // 512):
        a[p, :8] = np.random.permutation(np.resize(levels, 8))
        for g in range(8):
            far = levels[np.abs(levels - a[p, g]) >= 10]
            a[p, g + 8] = far[np.random.randint(len(far))]
    return np.exp2(a.ravel()).repeat(32)


BF16 = ml_dtypes.bfloat16


def bf(x):
    return np.asarray(x, np.float32).astype(BF16)


def f64(x):
    return np.asarray(x).astype(np.float64)


E, LMAX, MMAX, CIN, COUT = 128, 2, 2, 4096, 128
NS = [LMAX + 1 - m for m in range(MMAX + 1)]
NC = NS[0] + sum(2 * n for n in NS[1:])


def setup_inputs():
    ss = [mx_kscale(n * CIN) for n in NS]
    sx = np.concatenate([ss[0].reshape(NS[0], CIN)] + [np.tile(ss[m].reshape(NS[m], CIN), (2, 1)) for m in range(1, MMAX + 1)], axis=0)
    x = np.random.standard_normal((E, NC, CIN)) * sx
    W0 = np.random.standard_normal((NS[0] * COUT, NS[0] * CIN)) / np.sqrt(NS[0] * CIN) / ss[0][None, :]
    b0 = np.random.standard_normal(NS[0] * COUT) * 0.3
    W1 = np.random.standard_normal((2 * NS[1] * COUT, NS[1] * CIN)) / (np.sqrt(2.0) * np.sqrt(NS[1] * CIN)) / ss[1][None, :]
    W2 = np.random.standard_normal((2 * NS[2] * COUT, NS[2] * CIN)) / (np.sqrt(2.0) * np.sqrt(NS[2] * CIN)) / ss[2][None, :]
    return {"x": bf(x), "W0": bf(W0), "b0": bf(b0), "W1": bf(W1), "W2": bf(W2)}


def reference(x, W0, b0, W1, W2):
    x = f64(x)
    Wm = [f64(W1), f64(W2)]
    outs = []
    x0 = x[:, :LMAX + 1].reshape(E, (LMAX + 1) * CIN)
    y0 = (mxq(x0, 1, "e4m3") @ mxq(f64(W0), 1, "e4m3").T) + f64(b0)
    outs.append(y0.reshape(E, LMAX + 1, COUT))
    offset = LMAX + 1
    for m in range(1, MMAX + 1):
        n = LMAX + 1 - m
        xm = x[:, offset:offset + 2 * n].reshape(E, 2, n * CIN)
        offset += 2 * n
        ym = mxq(xm, 2, "e4m3") @ mxq(Wm[m - 1], 1, "e4m3").T
        of = n * COUT
        x_r, x_i = ym[..., :of], ym[..., of:]
        pos = x_r[:, 0] - x_i[:, 1]
        neg = x_r[:, 1] + x_i[:, 0]
        outs.append(pos.reshape(E, n, COUT))
        outs.append(neg.reshape(E, n, COUT))
    return np.concatenate(outs, axis=1)

@@ -1,0 +1,199 @@
+from contextlib import ExitStack
+
+import concourse.masks as masks
+import concourse.mybir as mybir
+
+F32 = mybir.dt.float32
+BF16 = mybir.dt.bfloat16
+U32 = mybir.dt.uint32
+U8 = mybir.dt.uint8
+FP8X4 = mybir.dt.float8_e4m3fn_x4
+ADD = mybir.AluOpType.add
+SUBTRACT = mybir.AluOpType.subtract
+
+P = 128
+PACK = 4
+K_PASS = P * PACK
+HALVES = 2
+CIN = 4096
+COUT = 128
+BANK_F32 = 512
+BANK_PASSES = BANK_F32 // (HALVES * P)
+
+CHUNK_PASSES = 4
+CHUNK_K = CHUNK_PASSES * K_PASS
+RUN_PASSES = 2
+TILES_AHEAD = 18
+TRANSPOSE_BANKS = 6
+VECTOR_COPY_EVERY = 4
+
+FLOPS = 2 * P * (384 * 12288 + 2 * 512 * 8192 + 2 * 256 * 4096)
+
+
+def list_stages(x_flat, W0, W1, W2):
+    def weight_tiles(w, slab):
+        return [w[r : r + P, slab * CIN : (slab + 1) * CIN] for r in range(0, w.shape[0], P)]
+
+    def x_tile(component):
+        return x_flat[:, component * CIN : (component + 1) * CIN]
+
+    return [
+        dict(
+            slabs=[weight_tiles(W1, s) + [x_tile(3 + s), x_tile(5 + s)] for s in range(2)],
+            products=[(4, 0, 512), (5, 0, 512)],
+            out_col=3 * COUT,
+        ),
+        dict(
+            slabs=[weight_tiles(W0, s) + [x_tile(s)] for s in range(3)],
+            products=[(3, 0, 256), (3, 256, 128)],
+            out_col=0,
+        ),
+        dict(
+            slabs=[weight_tiles(W2, 0) + [x_tile(7), x_tile(8)]],
+            products=[(2, 0, 256), (3, 0, 256)],
+            out_col=7 * COUT,
+        ),
+    ]
+
+
+def tile_so2linear_k_kernel(tc, x, W0, b0, W1, W2, out):
+    nc = tc.nc
+    out_flat = out.rearrange("e c o -> e (c o)")
+    stages = list_stages(x.rearrange("e c k -> e (c k)"), W0, W1, W2)
+
+    chunks = []
+    for s, stage in enumerate(stages):
+        for slab in stage["slabs"]:
+            for k0 in range(0, CIN, CHUNK_K):
+                chunks.append((s, [view[:, k0 : k0 + CHUNK_K] for view in slab]))
+    first_chunk = [min(c for c, chunk in enumerate(chunks) if chunk[0] == s) for s in range(len(stages))]
+    last_chunk = [max(c for c, chunk in enumerate(chunks) if chunk[0] == s) for s in range(len(stages))]
+    tile_views = [view for (s, views) in chunks for view in views]
+
+    with ExitStack() as ctx:
+        const = ctx.enter_context(tc.tile_pool(name="const", bufs=1))
+        raw_pool = ctx.enter_context(tc.tile_pool(name="raw", bufs=TILES_AHEAD + 1))
+        grouped_pool = ctx.enter_context(tc.tile_pool(name="grouped", bufs=TRANSPOSE_BANKS))
+        quantised_pool = ctx.enter_context(tc.tile_pool(name="quantised", bufs=2))
+        bank_pool = ctx.enter_context(tc.psum_pool(name="banks", bufs=TRANSPOSE_BANKS))
+        sum_pool = ctx.enter_context(tc.psum_pool(name="sums", bufs=1))
+        ctx.enter_context(tc.manual_schedule())
+
+        identity = const.tile([P, P], F32)
+        masks.make_identity(nc, identity[:])
+        ones = const.tile([P, P], BF16)
+        nc.vector.memset(ones[:], 1.0)
+        bias_rows = const.tile([P, BANK_F32], BF16)
+        nc.vector.memset(bias_rows[:], 0.0)
+        nc.scalar.dma_start(out=bias_rows[0:1, 0 : 3 * COUT], in_=b0.rearrange("(o n) -> o n", o=1))
+        out_sb = const.tile([P, 9 * COUT], F32)
+
+        def load(j):
+            raw = raw_pool.tile([P, CHUNK_K], BF16, tag="raw")
+            nc.sync.dma_start(out=raw[:], in_=tile_views[j])
+            return raw
+
+        def quantise(grouped, codes, scales, g0, cols):
+            for i in range(BANK_PASSES):
+                nc.vector.quantize_mx(
+                    out=codes[:, g0 + i, cols].bitcast(FP8X4),
+                    scales=scales[:, g0 + i, cols],
+                    in_=grouped[:, i * K_PASS : (i + 1) * K_PASS],
+                )
+
+        def finish_with_bias(sums, col):
+            bias_bank = bank_pool.tile([P, BANK_F32], F32, tag="bank")
+            nc.tensor.matmul(out=bias_bank[:], lhsT=ones[:], rhs=bias_rows[:], start=True, stop=True)
+            bias = const.tile([P, 3 * COUT], F32)
+            nc.scalar.copy(out=bias[:], in_=bias_bank[:, 0 : 3 * COUT])
+            nc.vector.tensor_tensor(out=out_sb[:, col : col + 256], in0=sums[0][:], in1=bias[:, 0:256], op=ADD)
+            nc.vector.tensor_tensor(
+                out=out_sb[:, col + 256 : col + 384], in0=sums[1][:], in1=bias[:, 256:384], op=ADD
+            )
+            nc.sync.dma_start(out=out_flat[:, col : col + 384], in_=out_sb[:, col : col + 384])
+
+        def finish_complex(sums, n, col):
+            h = n // 2
+            from_xr = const.tile([P, n], F32, tag="from_xr")
+            nc.scalar.copy(out=from_xr[:], in_=sums[0][:])
+            nc.vector.tensor_tensor(
+                out=out_sb[:, col : col + h], in0=from_xr[:, 0:h], in1=sums[1][:, h:n], op=SUBTRACT
+            )
+            nc.vector.tensor_tensor(
+                out=out_sb[:, col + h : col + n], in0=from_xr[:, h:n], in1=sums[1][:, 0:h], op=ADD
+            )
+            nc.sync.dma_start(out=out_flat[:, col : col + n], in_=out_sb[:, col : col + n])
+
+        sums_of = {}
+
+        def multiply(c, codes, scales, g_first, g_count):
+            s = chunks[c][0]
+            products = stages[s]["products"]
+            if c == first_chunk[s] and g_first == 0:
+                sums_of[s] = [
+                    sum_pool.tile([P, n], F32, name="sum%d" % i, tag="sum%d" % i)
+                    for i, (x_index, w0, n) in enumerate(products)
+                ]
+            for acc, (x_index, w0, n) in zip(sums_of[s], products):
+                x_cols = slice(x_index * P, (x_index + 1) * P)
+                for g in range(g_first, g_first + g_count):
+                    nc.tensor.matmul_mx(
+                        out=acc[:],
+                        lhsT=codes[:, g, x_cols].bitcast(FP8X4),
+                        lhsT_scale=scales[:, g, x_cols],
+                        rhs=codes[:, g, w0 : w0 + n].bitcast(FP8X4),
+                        rhs_scale=scales[:, g, w0 : w0 + n],
+                        start=(c == first_chunk[s] and g == 0),
+                        stop=(c == last_chunk[s] and g == CHUNK_PASSES - 1),
+                    )
+            if c == last_chunk[s] and g_first + g_count == CHUNK_PASSES:
+                if stages[s]["out_col"] == 0:
+                    finish_with_bias(sums_of[s], 0)
+                else:
+                    finish_complex(sums_of[s], products[0][2], stages[s]["out_col"])
+
+        raw_of = {}
+        for j in range(TILES_AHEAD):
+            raw_of[j] = load(j)
+
+        j = 0
+        banks_done = 0
+        copied = None
+        before = None
+        for c, (s, views) in enumerate(chunks):
+            columns = len(views) * P
+            codes = quantised_pool.tile([P, CHUNK_PASSES, columns], U32, tag="codes", align_bytes=64)
+            scales = quantised_pool.tile([P, CHUNK_PASSES, columns], U8, tag="scales", align_bytes=64)
+            run_banks = len(views) * RUN_PASSES // BANK_PASSES
+            banks_in_chunk = 0
+
+            for t in range(len(views)):
+                if j + TILES_AHEAD < len(tile_views):
+                    raw_of[j + TILES_AHEAD] = load(j + TILES_AHEAD)
+                words = raw_of[j][:].bitcast(F32)
+                j += 1
+                for g0 in range(0, CHUNK_PASSES, BANK_PASSES):
+                    bank = bank_pool.tile([P, BANK_F32], F32, tag="bank")
+                    for b in range(BANK_PASSES * HALVES):
+                        g, u = g0 + b // HALVES, b % HALVES
+                        in_words = words[:, g * HALVES * P + u : (g + 1) * HALVES * P : HALVES]
+                        nc.tensor.transpose(bank[:, b * P : (b + 1) * P], in_words, identity[:])
+                    grouped = grouped_pool.tile([P, BANK_PASSES * K_PASS], BF16, tag="grouped", align_bytes=64)
+                    copy_out = grouped[:].bitcast(F32).rearrange("p (i r u) -> p i r u", i=BANK_PASSES, u=HALVES)
+                    copy_in = bank[:].rearrange("p (i u r) -> p i r u", i=BANK_PASSES, u=HALVES)
+                    if banks_done % VECTOR_COPY_EVERY == VECTOR_COPY_EVERY - 1:
+                        nc.vector.tensor_copy(out=copy_out, in_=copy_in)
+                    else:
+                        nc.scalar.copy(out=copy_out, in_=copy_in)
+                    banks_done += 1
+                    if copied is not None:
+                        quantise(*copied)
+                    copied = (grouped, codes, scales, g0, slice(t * P, (t + 1) * P))
+
+                    banks_in_chunk += 1
+                    if before is not None and banks_in_chunk % run_banks == 0:
+                        multiply(*before, (banks_in_chunk // run_banks - 1) * RUN_PASSES, RUN_PASSES)
+            before = (c, codes, scales)
+
+        quantise(*copied)
+        multiply(*before, 0, CHUNK_PASSES)

@@ -18,14 +18,15 @@ HALVES = 2
 CIN = 4096
 COUT = 128
 BANK_F32 = 512
-BANK_PASSES = BANK_F32 // (HALVES * P)
+BANK_TILES = BANK_F32 // (HALVES * P)
 
 CHUNK_PASSES = 4
 CHUNK_K = CHUNK_PASSES * K_PASS
 RUN_PASSES = 2
 TILES_AHEAD = 18
 TRANSPOSE_BANKS = 6
-VECTOR_COPY_EVERY = 4
+VECTOR_COPY_EVERY = 8
+SORT_EVERY = 2
 
 FLOPS = 2 * P * (384 * 12288 + 2 * 512 * 8192 + 2 * 256 * 4096)
 
@@ -72,7 +73,8 @@ def tile_so2linear_k_kernel(tc, x, W0, b0, W1, W2, out):
 
     with ExitStack() as ctx:
         const = ctx.enter_context(tc.tile_pool(name="const", bufs=1))
-        raw_pool = ctx.enter_context(tc.tile_pool(name="raw", bufs=TILES_AHEAD + 1))
+        raw_pool = ctx.enter_context(tc.tile_pool(name="raw", bufs=TILES_AHEAD + BANK_TILES))
+        sorted_pool = ctx.enter_context(tc.tile_pool(name="sorted", bufs=3))
         grouped_pool = ctx.enter_context(tc.tile_pool(name="grouped", bufs=TRANSPOSE_BANKS))
         quantised_pool = ctx.enter_context(tc.tile_pool(name="quantised", bufs=2))
         bank_pool = ctx.enter_context(tc.psum_pool(name="banks", bufs=TRANSPOSE_BANKS))
@@ -93,13 +95,19 @@ def tile_so2linear_k_kernel(tc, x, W0, b0, W1, W2, out):
             nc.sync.dma_start(out=raw[:], in_=tile_views[j])
             return raw
 
-        def quantise(grouped, codes, scales, g0, cols):
-            for i in range(BANK_PASSES):
-                nc.vector.quantize_mx(
-                    out=codes[:, g0 + i, cols].bitcast(FP8X4),
-                    scales=scales[:, g0 + i, cols],
-                    in_=grouped[:, i * K_PASS : (i + 1) * K_PASS],
-                )
+        def sort_words(raw):
+            tile = sorted_pool.tile([P, CHUNK_PASSES, HALVES, P], F32, tag="sorted")
+            words = raw[:].bitcast(F32).rearrange("p (g w u) -> p g u w", g=CHUNK_PASSES, u=HALVES)
+            nc.vector.tensor_copy(out=tile[:], in_=words)
+            return tile
+
+        def halves_of(j):
+            if j % SORT_EVERY == 0:
+                return sort_words(raw_of[j])[:]
+            return raw_of[j][:].bitcast(F32).rearrange("p (g w u) -> p g u w", g=CHUNK_PASSES, u=HALVES)
+
+        def quantise(grouped, codes, scales, g, cols):
+            nc.vector.quantize_mx(out=codes[:, g, cols].bitcast(FP8X4), scales=scales[:, g, cols], in_=grouped[:])
 
         def finish_with_bias(sums, col):
             bias_bank = bank_pool.tile([P, BANK_F32], F32, tag="bank")
@@ -156,6 +164,7 @@ def tile_so2linear_k_kernel(tc, x, W0, b0, W1, W2, out):
         for j in range(TILES_AHEAD):
             raw_of[j] = load(j)
 
+        pair = [halves_of(0), halves_of(1)]
         j = 0
         banks_done = 0
         copied = None
@@ -164,23 +173,22 @@ def tile_so2linear_k_kernel(tc, x, W0, b0, W1, W2, out):
             columns = len(views) * P
             codes = quantised_pool.tile([P, CHUNK_PASSES, columns], U32, tag="codes", align_bytes=64)
             scales = quantised_pool.tile([P, CHUNK_PASSES, columns], U8, tag="scales", align_bytes=64)
-            run_banks = len(views) * RUN_PASSES // BANK_PASSES
+            run_banks = len(views) * RUN_PASSES // BANK_TILES
             banks_in_chunk = 0
 
-            for t in range(len(views)):
-                if j + TILES_AHEAD < len(tile_views):
-                    raw_of[j + TILES_AHEAD] = load(j + TILES_AHEAD)
-                words = raw_of[j][:].bitcast(F32)
-                j += 1
-                for g0 in range(0, CHUNK_PASSES, BANK_PASSES):
+            for t in range(0, len(views), BANK_TILES):
+                for i in range(j + TILES_AHEAD, min(j + TILES_AHEAD + BANK_TILES, len(tile_views))):
+                    raw_of[i] = load(i)
+                j += BANK_TILES
+                next_pair = [halves_of(i) for i in range(j, min(j + BANK_TILES, len(tile_views)))]
+                for g in range(CHUNK_PASSES):
                     bank = bank_pool.tile([P, BANK_F32], F32, tag="bank")
-                    for b in range(BANK_PASSES * HALVES):
-                        g, u = g0 + b // HALVES, b % HALVES
-                        in_words = words[:, g * HALVES * P + u : (g + 1) * HALVES * P : HALVES]
+                    for b in range(BANK_TILES * HALVES):
+                        in_words = pair[b // HALVES][:, g, b % HALVES, :]
                         nc.tensor.transpose(bank[:, b * P : (b + 1) * P], in_words, identity[:])
-                    grouped = grouped_pool.tile([P, BANK_PASSES * K_PASS], BF16, tag="grouped", align_bytes=64)
-                    copy_out = grouped[:].bitcast(F32).rearrange("p (i r u) -> p i r u", i=BANK_PASSES, u=HALVES)
-                    copy_in = bank[:].rearrange("p (i u r) -> p i r u", i=BANK_PASSES, u=HALVES)
+                    grouped = grouped_pool.tile([P, BANK_TILES * K_PASS], BF16, tag="grouped", align_bytes=64)
+                    copy_out = grouped[:].bitcast(F32).rearrange("p (i r u) -> p i r u", i=BANK_TILES, u=HALVES)
+                    copy_in = bank[:].rearrange("p (i u r) -> p i r u", i=BANK_TILES, u=HALVES)
                     if banks_done % VECTOR_COPY_EVERY == VECTOR_COPY_EVERY - 1:
                         nc.vector.tensor_copy(out=copy_out, in_=copy_in)
                     else:
@@ -188,11 +196,12 @@ def tile_so2linear_k_kernel(tc, x, W0, b0, W1, W2, out):
                     banks_done += 1
                     if copied is not None:
                         quantise(*copied)
-                    copied = (grouped, codes, scales, g0, slice(t * P, (t + 1) * P))
+                    copied = (grouped, codes, scales, g, slice(t * P, (t + BANK_TILES) * P))
 
                     banks_in_chunk += 1
                     if before is not None and banks_in_chunk % run_banks == 0:
                         multiply(*before, (banks_in_chunk // run_banks - 1) * RUN_PASSES, RUN_PASSES)
+                pair = next_pair
             before = (c, codes, scales)
 
         quantise(*copied)

@@ -25,6 +25,7 @@ CHUNK_K = CHUNK_PASSES * K_PASS
 RUN_PASSES = 2
 TILES_AHEAD = 18
 TRANSPOSE_BANKS = 6
+QUANTISE_LAG = 3
 VECTOR_COPY_EVERY = 8
 SORT_EVERY = 2
 
@@ -45,14 +46,14 @@ def list_stages(x_flat, W0, W1, W2):
             out_col=3 * COUT,
         ),
         dict(
-            slabs=[weight_tiles(W0, s) + [x_tile(s)] for s in range(3)],
-            products=[(3, 0, 256), (3, 256, 128)],
-            out_col=0,
-        ),
-        dict(
             slabs=[weight_tiles(W2, 0) + [x_tile(7), x_tile(8)]],
             products=[(2, 0, 256), (3, 0, 256)],
             out_col=7 * COUT,
+        ),
+        dict(
+            slabs=[weight_tiles(W0, s) + [x_tile(s)] for s in range(3)],
+            products=[(3, 0, 256), (3, 256, 128)],
+            out_col=0,
         ),
     ]
 
@@ -75,7 +76,7 @@ def tile_so2linear_k_kernel(tc, x, W0, b0, W1, W2, out):
         const = ctx.enter_context(tc.tile_pool(name="const", bufs=1))
         raw_pool = ctx.enter_context(tc.tile_pool(name="raw", bufs=TILES_AHEAD + BANK_TILES))
         sorted_pool = ctx.enter_context(tc.tile_pool(name="sorted", bufs=3))
-        grouped_pool = ctx.enter_context(tc.tile_pool(name="grouped", bufs=TRANSPOSE_BANKS))
+        grouped_pool = ctx.enter_context(tc.tile_pool(name="grouped", bufs=4))
         quantised_pool = ctx.enter_context(tc.tile_pool(name="quantised", bufs=2))
         bank_pool = ctx.enter_context(tc.psum_pool(name="banks", bufs=TRANSPOSE_BANKS))
         sum_pool = ctx.enter_context(tc.psum_pool(name="sums", bufs=1))
@@ -88,7 +89,16 @@ def tile_so2linear_k_kernel(tc, x, W0, b0, W1, W2, out):
         bias_rows = const.tile([P, BANK_F32], BF16)
         nc.vector.memset(bias_rows[:], 0.0)
         nc.scalar.dma_start(out=bias_rows[0:1, 0 : 3 * COUT], in_=b0.rearrange("(o n) -> o n", o=1))
+        bias = const.tile([P, 3 * COUT], F32)
         out_sb = const.tile([P, 9 * COUT], F32)
+
+        def load_first_pair():
+            raws = [raw_pool.tile([P, CHUNK_K], BF16, name="raw", tag="raw") for i in range(BANK_TILES)]
+            for g in range(CHUNK_PASSES):
+                k = slice(g * K_PASS, (g + 1) * K_PASS)
+                for raw, view in zip(raws, tile_views):
+                    nc.sync.dma_start(out=raw[:, k], in_=view[:, k])
+            return raws
 
         def load(j):
             raw = raw_pool.tile([P, CHUNK_K], BF16, tag="raw")
@@ -102,18 +112,19 @@ def tile_so2linear_k_kernel(tc, x, W0, b0, W1, W2, out):
             return tile
 
         def halves_of(j):
-            if j % SORT_EVERY == 0:
+            if j >= len(chunks[0][1]) and j % SORT_EVERY == 0:
                 return sort_words(raw_of[j])[:]
             return raw_of[j][:].bitcast(F32).rearrange("p (g w u) -> p g u w", g=CHUNK_PASSES, u=HALVES)
 
         def quantise(grouped, codes, scales, g, cols):
-            nc.vector.quantize_mx(out=codes[:, g, cols].bitcast(FP8X4), scales=scales[:, g, cols], in_=grouped[:])
+            nc.vector.quantize_mx(out=codes[:, g, cols].bitcast(FP8X4), scales=scales[:, g, cols], in_=grouped)
 
-        def finish_with_bias(sums, col):
+        def spread_bias():
             bias_bank = bank_pool.tile([P, BANK_F32], F32, tag="bank")
             nc.tensor.matmul(out=bias_bank[:], lhsT=ones[:], rhs=bias_rows[:], start=True, stop=True)
-            bias = const.tile([P, 3 * COUT], F32)
             nc.scalar.copy(out=bias[:], in_=bias_bank[:, 0 : 3 * COUT])
+
+        def finish_with_bias(sums, col):
             nc.vector.tensor_tensor(out=out_sb[:, col : col + 256], in0=sums[0][:], in1=bias[:, 0:256], op=ADD)
             nc.vector.tensor_tensor(
                 out=out_sb[:, col + 256 : col + 384], in0=sums[1][:], in1=bias[:, 256:384], op=ADD
@@ -142,9 +153,9 @@ def tile_so2linear_k_kernel(tc, x, W0, b0, W1, W2, out):
                     sum_pool.tile([P, n], F32, name="sum%d" % i, tag="sum%d" % i)
                     for i, (x_index, w0, n) in enumerate(products)
                 ]
-            for acc, (x_index, w0, n) in zip(sums_of[s], products):
-                x_cols = slice(x_index * P, (x_index + 1) * P)
-                for g in range(g_first, g_first + g_count):
+            for g in range(g_first, g_first + g_count):
+                for acc, (x_index, w0, n) in zip(sums_of[s], products):
+                    x_cols = slice(x_index * P, (x_index + 1) * P)
                     nc.tensor.matmul_mx(
                         out=acc[:],
                         lhsT=codes[:, g, x_cols].bitcast(FP8X4),
@@ -160,14 +171,14 @@ def tile_so2linear_k_kernel(tc, x, W0, b0, W1, W2, out):
                 else:
                     finish_complex(sums_of[s], products[0][2], stages[s]["out_col"])
 
-        raw_of = {}
-        for j in range(TILES_AHEAD):
+        raw_of = dict(enumerate(load_first_pair()))
+        for j in range(BANK_TILES, TILES_AHEAD):
             raw_of[j] = load(j)
 
         pair = [halves_of(0), halves_of(1)]
         j = 0
         banks_done = 0
-        copied = None
+        copied = []
         before = None
         for c, (s, views) in enumerate(chunks):
             columns = len(views) * P
@@ -181,28 +192,31 @@ def tile_so2linear_k_kernel(tc, x, W0, b0, W1, W2, out):
                     raw_of[i] = load(i)
                 j += BANK_TILES
                 next_pair = [halves_of(i) for i in range(j, min(j + BANK_TILES, len(tile_views)))]
+                grouped = grouped_pool.tile([P, CHUNK_PASSES, BANK_TILES * K_PASS], BF16, tag="grouped", align_bytes=64)
                 for g in range(CHUNK_PASSES):
                     bank = bank_pool.tile([P, BANK_F32], F32, tag="bank")
                     for b in range(BANK_TILES * HALVES):
                         in_words = pair[b // HALVES][:, g, b % HALVES, :]
                         nc.tensor.transpose(bank[:, b * P : (b + 1) * P], in_words, identity[:])
-                    grouped = grouped_pool.tile([P, BANK_TILES * K_PASS], BF16, tag="grouped", align_bytes=64)
-                    copy_out = grouped[:].bitcast(F32).rearrange("p (i r u) -> p i r u", i=BANK_TILES, u=HALVES)
+                    copy_out = grouped[:, g, :].bitcast(F32).rearrange("p (i r u) -> p i r u", i=BANK_TILES, u=HALVES)
                     copy_in = bank[:].rearrange("p (i u r) -> p i r u", i=BANK_TILES, u=HALVES)
                     if banks_done % VECTOR_COPY_EVERY == VECTOR_COPY_EVERY - 1:
                         nc.vector.tensor_copy(out=copy_out, in_=copy_in)
                     else:
                         nc.scalar.copy(out=copy_out, in_=copy_in)
                     banks_done += 1
-                    if copied is not None:
-                        quantise(*copied)
-                    copied = (grouped, codes, scales, g, slice(t * P, (t + BANK_TILES) * P))
+                    copied.append((grouped[:, g, :], codes, scales, g, slice(t * P, (t + BANK_TILES) * P)))
+                    if len(copied) > QUANTISE_LAG:
+                        quantise(*copied[-1 - QUANTISE_LAG])
 
                     banks_in_chunk += 1
                     if before is not None and banks_in_chunk % run_banks == 0:
                         multiply(*before, (banks_in_chunk // run_banks - 1) * RUN_PASSES, RUN_PASSES)
                 pair = next_pair
             before = (c, codes, scales)
+            if s == 0 and c == last_chunk[s]:
+                spread_bias()
 
-        quantise(*copied)
+        for bank in copied[-QUANTISE_LAG:]:
+            quantise(*bank)
         multiply(*before, 0, CHUNK_PASSES)

@@ -25,9 +25,10 @@ CHUNK_K = CHUNK_PASSES * K_PASS
 RUN_PASSES = 2
 TILES_AHEAD = 18
 TRANSPOSE_BANKS = 6
-QUANTISE_LAG = 3
-VECTOR_COPY_EVERY = 8
-SORT_EVERY = 2
+QUANTISE_LAG = 2
+PASS_LAG = 4
+SORT_PERIOD = 3
+SORTED_AHEAD = 3
 
 FLOPS = 2 * P * (384 * 12288 + 2 * 512 * 8192 + 2 * 256 * 4096)
 
@@ -75,9 +76,9 @@ def tile_so2linear_k_kernel(tc, x, W0, b0, W1, W2, out):
     with ExitStack() as ctx:
         const = ctx.enter_context(tc.tile_pool(name="const", bufs=1))
         raw_pool = ctx.enter_context(tc.tile_pool(name="raw", bufs=TILES_AHEAD + BANK_TILES))
-        sorted_pool = ctx.enter_context(tc.tile_pool(name="sorted", bufs=3))
+        sorted_pool = ctx.enter_context(tc.tile_pool(name="sorted", bufs=6))
         grouped_pool = ctx.enter_context(tc.tile_pool(name="grouped", bufs=4))
-        quantised_pool = ctx.enter_context(tc.tile_pool(name="quantised", bufs=2))
+        quantised_pool = ctx.enter_context(tc.tile_pool(name="quantised", bufs=3))
         bank_pool = ctx.enter_context(tc.psum_pool(name="banks", bufs=TRANSPOSE_BANKS))
         sum_pool = ctx.enter_context(tc.psum_pool(name="sums", bufs=1))
         ctx.enter_context(tc.manual_schedule())
@@ -111,10 +112,15 @@ def tile_so2linear_k_kernel(tc, x, W0, b0, W1, W2, out):
             nc.vector.tensor_copy(out=tile[:], in_=words)
             return tile
 
-        def halves_of(j):
-            if j >= len(chunks[0][1]) and j % SORT_EVERY == 0:
-                return sort_words(raw_of[j])[:]
-            return raw_of[j][:].bitcast(F32).rearrange("p (g w u) -> p g u w", g=CHUNK_PASSES, u=HALVES)
+        halves_of = {}
+
+        def prepare(j):
+            if j < len(tile_views):
+                if j >= len(chunks[0][1]) and j % SORT_PERIOD != SORT_PERIOD - 1:
+                    halves_of[j] = sort_words(raw_of[j])[:]
+                else:
+                    words = raw_of[j][:].bitcast(F32)
+                    halves_of[j] = words.rearrange("p (g w u) -> p g u w", g=CHUNK_PASSES, u=HALVES)
 
         def quantise(grouped, codes, scales, g, cols):
             nc.vector.quantize_mx(out=codes[:, g, cols].bitcast(FP8X4), scales=scales[:, g, cols], in_=grouped)
@@ -175,48 +181,48 @@ def tile_so2linear_k_kernel(tc, x, W0, b0, W1, W2, out):
         for j in range(BANK_TILES, TILES_AHEAD):
             raw_of[j] = load(j)
 
-        pair = [halves_of(0), halves_of(1)]
+        for j in range(SORTED_AHEAD):
+            prepare(j)
+
         j = 0
         banks_done = 0
         copied = []
-        before = None
+        runs = []
+        runs_done = 0
         for c, (s, views) in enumerate(chunks):
             columns = len(views) * P
             codes = quantised_pool.tile([P, CHUNK_PASSES, columns], U32, tag="codes", align_bytes=64)
             scales = quantised_pool.tile([P, CHUNK_PASSES, columns], U8, tag="scales", align_bytes=64)
-            run_banks = len(views) * RUN_PASSES // BANK_TILES
-            banks_in_chunk = 0
-
             for t in range(0, len(views), BANK_TILES):
                 for i in range(j + TILES_AHEAD, min(j + TILES_AHEAD + BANK_TILES, len(tile_views))):
                     raw_of[i] = load(i)
-                j += BANK_TILES
-                next_pair = [halves_of(i) for i in range(j, min(j + BANK_TILES, len(tile_views)))]
                 grouped = grouped_pool.tile([P, CHUNK_PASSES, BANK_TILES * K_PASS], BF16, tag="grouped", align_bytes=64)
                 for g in range(CHUNK_PASSES):
+                    if g % 2 == 0:
+                        prepare(j + SORTED_AHEAD + g // 2)
                     bank = bank_pool.tile([P, BANK_F32], F32, tag="bank")
                     for b in range(BANK_TILES * HALVES):
-                        in_words = pair[b // HALVES][:, g, b % HALVES, :]
+                        in_words = halves_of[j + b // HALVES][:, g, b % HALVES, :]
                         nc.tensor.transpose(bank[:, b * P : (b + 1) * P], in_words, identity[:])
                     copy_out = grouped[:, g, :].bitcast(F32).rearrange("p (i r u) -> p i r u", i=BANK_TILES, u=HALVES)
                     copy_in = bank[:].rearrange("p (i u r) -> p i r u", i=BANK_TILES, u=HALVES)
-                    if banks_done % VECTOR_COPY_EVERY == VECTOR_COPY_EVERY - 1:
-                        nc.vector.tensor_copy(out=copy_out, in_=copy_in)
-                    else:
-                        nc.scalar.copy(out=copy_out, in_=copy_in)
+                    nc.scalar.copy(out=copy_out, in_=copy_in)
                     banks_done += 1
                     copied.append((grouped[:, g, :], codes, scales, g, slice(t * P, (t + BANK_TILES) * P)))
                     if len(copied) > QUANTISE_LAG:
                         quantise(*copied[-1 - QUANTISE_LAG])
-
-                    banks_in_chunk += 1
-                    if before is not None and banks_in_chunk % run_banks == 0:
-                        multiply(*before, (banks_in_chunk // run_banks - 1) * RUN_PASSES, RUN_PASSES)
-                pair = next_pair
-            before = (c, codes, scales)
+                    if runs_done < len(runs) and runs[runs_done][0] <= banks_done:
+                        multiply(*runs[runs_done][1])
+                        runs_done += 1
+                j += BANK_TILES
+            next_banks = len(chunks[min(c + 1, len(chunks) - 1)][1]) // BANK_TILES * CHUNK_PASSES
+            for g in range(0, CHUNK_PASSES, RUN_PASSES):
+                due = banks_done + PASS_LAG + next_banks * (g + RUN_PASSES) // CHUNK_PASSES
+                runs.append((due, (c, codes, scales, g, RUN_PASSES)))
             if s == 0 and c == last_chunk[s]:
                 spread_bias()
 
         for bank in copied[-QUANTISE_LAG:]:
             quantise(*bank)
-        multiply(*before, 0, CHUNK_PASSES)
+        for due, passes in runs[runs_done:]:
+            multiply(*passes)

@@ -25,8 +25,9 @@ CHUNK_K = CHUNK_PASSES * K_PASS
 RUN_PASSES = 2
 TILES_AHEAD = 18
 TRANSPOSE_BANKS = 6
-QUANTISE_LAG = 2
+QUANTISE_BANKS = 2
 PASS_LAG = 4
+VECTOR_COPY_EVERY = 16
 SORT_PERIOD = 3
 SORTED_AHEAD = 3
 
@@ -42,18 +43,18 @@ def list_stages(x_flat, W0, W1, W2):
 
     return [
         dict(
-            slabs=[weight_tiles(W1, s) + [x_tile(3 + s), x_tile(5 + s)] for s in range(2)],
-            products=[(4, 0, 512), (5, 0, 512)],
+            slabs=[[weight_tiles(W1, s), [x_tile(3 + s), x_tile(5 + s)]] for s in range(2)],
+            products=[((1, 0), (0, 0), 512), ((1, 1), (0, 0), 512)],
             out_col=3 * COUT,
         ),
         dict(
-            slabs=[weight_tiles(W2, 0) + [x_tile(7), x_tile(8)]],
-            products=[(2, 0, 256), (3, 0, 256)],
+            slabs=[[weight_tiles(W2, 0), [x_tile(7), x_tile(8)]]],
+            products=[((1, 0), (0, 0), 256), ((1, 1), (0, 0), 256)],
             out_col=7 * COUT,
         ),
         dict(
-            slabs=[weight_tiles(W0, s) + [x_tile(s)] for s in range(3)],
-            products=[(3, 0, 256), (3, 256, 128)],
+            slabs=[[weight_tiles(W0, s)[:2], weight_tiles(W0, s)[2:] + [x_tile(s)]] for s in range(3)],
+            products=[((1, 1), (0, 0), 256), ((1, 1), (1, 0), 128)],
             out_col=0,
         ),
     ]
@@ -68,10 +69,11 @@ def tile_so2linear_k_kernel(tc, x, W0, b0, W1, W2, out):
     for s, stage in enumerate(stages):
         for slab in stage["slabs"]:
             for k0 in range(0, CIN, CHUNK_K):
-                chunks.append((s, [view[:, k0 : k0 + CHUNK_K] for view in slab]))
+                chunks.append((s, [[view[:, k0 : k0 + CHUNK_K] for view in group] for group in slab]))
     first_chunk = [min(c for c, chunk in enumerate(chunks) if chunk[0] == s) for s in range(len(stages))]
     last_chunk = [max(c for c, chunk in enumerate(chunks) if chunk[0] == s) for s in range(len(stages))]
-    tile_views = [view for (s, views) in chunks for view in views]
+    tile_views = [view for (s, groups) in chunks for group in groups for view in group]
+    chunk_tiles = [sum(len(group) for group in groups) for (s, groups) in chunks]
 
     with ExitStack() as ctx:
         const = ctx.enter_context(tc.tile_pool(name="const", bufs=1))
@@ -116,14 +118,27 @@ def tile_so2linear_k_kernel(tc, x, W0, b0, W1, W2, out):
 
         def prepare(j):
             if j < len(tile_views):
-                if j >= len(chunks[0][1]) and j % SORT_PERIOD != SORT_PERIOD - 1:
+                if j >= chunk_tiles[0] and j % SORT_PERIOD != SORT_PERIOD - 1:
                     halves_of[j] = sort_words(raw_of[j])[:]
                 else:
                     words = raw_of[j][:].bitcast(F32)
                     halves_of[j] = words.rearrange("p (g w u) -> p g u w", g=CHUNK_PASSES, u=HALVES)
 
-        def quantise(grouped, codes, scales, g, cols):
-            nc.vector.quantize_mx(out=codes[:, g, cols].bitcast(FP8X4), scales=scales[:, g, cols], in_=grouped)
+        def quantise(grouped, codes, scales, g, first, last=False):
+            columns = BANK_TILES * P
+            if codes[:].shape[2] == columns and not last:
+                nc.vector.quantize_mx(
+                    out=codes[:, g : g + 2, :].rearrange("p g n -> p (g n)").bitcast(FP8X4),
+                    scales=scales[:, g : g + 2, :].rearrange("p g n -> p (g n)"),
+                    in_=grouped[:, g : g + 2, :].rearrange("p g n -> p (g n)"),
+                )
+            else:
+                for i in range(g, g + 2):
+                    nc.vector.quantize_mx(
+                        out=codes[:, i, first : first + columns].bitcast(FP8X4),
+                        scales=scales[:, i, first : first + columns],
+                        in_=grouped[:, i, :],
+                    )
 
         def spread_bias():
             bias_bank = bank_pool.tile([P, BANK_F32], F32, tag="bank")
@@ -157,17 +172,18 @@ def tile_so2linear_k_kernel(tc, x, W0, b0, W1, W2, out):
             if c == first_chunk[s] and g_first == 0:
                 sums_of[s] = [
                     sum_pool.tile([P, n], F32, name="sum%d" % i, tag="sum%d" % i)
-                    for i, (x_index, w0, n) in enumerate(products)
+                    for i, (x_tile, w_tile, n) in enumerate(products)
                 ]
             for g in range(g_first, g_first + g_count):
-                for acc, (x_index, w0, n) in zip(sums_of[s], products):
+                for acc, ((x_group, x_index), (w_group, w_index), n) in zip(sums_of[s], products):
                     x_cols = slice(x_index * P, (x_index + 1) * P)
+                    w_cols = slice(w_index * P, w_index * P + n)
                     nc.tensor.matmul_mx(
                         out=acc[:],
-                        lhsT=codes[:, g, x_cols].bitcast(FP8X4),
-                        lhsT_scale=scales[:, g, x_cols],
-                        rhs=codes[:, g, w0 : w0 + n].bitcast(FP8X4),
-                        rhs_scale=scales[:, g, w0 : w0 + n],
+                        lhsT=codes[x_group][:, g, x_cols].bitcast(FP8X4),
+                        lhsT_scale=scales[x_group][:, g, x_cols],
+                        rhs=codes[w_group][:, g, w_cols].bitcast(FP8X4),
+                        rhs_scale=scales[w_group][:, g, w_cols],
                         start=(c == first_chunk[s] and g == 0),
                         stop=(c == last_chunk[s] and g == CHUNK_PASSES - 1),
                     )
@@ -189,40 +205,47 @@ def tile_so2linear_k_kernel(tc, x, W0, b0, W1, W2, out):
         copied = []
         runs = []
         runs_done = 0
-        for c, (s, views) in enumerate(chunks):
-            columns = len(views) * P
-            codes = quantised_pool.tile([P, CHUNK_PASSES, columns], U32, tag="codes", align_bytes=64)
-            scales = quantised_pool.tile([P, CHUNK_PASSES, columns], U8, tag="scales", align_bytes=64)
-            for t in range(0, len(views), BANK_TILES):
-                for i in range(j + TILES_AHEAD, min(j + TILES_AHEAD + BANK_TILES, len(tile_views))):
-                    raw_of[i] = load(i)
+        for c, (s, groups) in enumerate(chunks):
+            codes, scales = [], []
+            for i, group in enumerate(groups):
+                shape = [P, CHUNK_PASSES, len(group) * P]
+                tag = "%d_%d" % (i, len(group))
+                codes.append(quantised_pool.tile(shape, U32, name="codes" + tag, tag="codes" + tag, align_bytes=64))
+                scales.append(quantised_pool.tile(shape, U8, name="scales" + tag, tag="scales" + tag, align_bytes=64))
+            pairs = [(i, t) for i, group in enumerate(groups) for t in range(0, len(group), BANK_TILES)]
+            for i, t in pairs:
+                for tile in range(j + TILES_AHEAD, min(j + TILES_AHEAD + BANK_TILES, len(tile_views))):
+                    raw_of[tile] = load(tile)
                 grouped = grouped_pool.tile([P, CHUNK_PASSES, BANK_TILES * K_PASS], BF16, tag="grouped", align_bytes=64)
                 for g in range(CHUNK_PASSES):
-                    if g % 2 == 0:
-                        prepare(j + SORTED_AHEAD + g // 2)
+                    if g % QUANTISE_BANKS == 0:
+                        prepare(j + SORTED_AHEAD + g // QUANTISE_BANKS)
                     bank = bank_pool.tile([P, BANK_F32], F32, tag="bank")
                     for b in range(BANK_TILES * HALVES):
                         in_words = halves_of[j + b // HALVES][:, g, b % HALVES, :]
                         nc.tensor.transpose(bank[:, b * P : (b + 1) * P], in_words, identity[:])
                     copy_out = grouped[:, g, :].bitcast(F32).rearrange("p (i r u) -> p i r u", i=BANK_TILES, u=HALVES)
                     copy_in = bank[:].rearrange("p (i u r) -> p i r u", i=BANK_TILES, u=HALVES)
-                    nc.scalar.copy(out=copy_out, in_=copy_in)
+                    if banks_done % VECTOR_COPY_EVERY == VECTOR_COPY_EVERY - 1:
+                        nc.vector.tensor_copy(out=copy_out, in_=copy_in)
+                    else:
+                        nc.scalar.copy(out=copy_out, in_=copy_in)
                     banks_done += 1
-                    copied.append((grouped[:, g, :], codes, scales, g, slice(t * P, (t + BANK_TILES) * P)))
-                    if len(copied) > QUANTISE_LAG:
-                        quantise(*copied[-1 - QUANTISE_LAG])
+                    if g % QUANTISE_BANKS == QUANTISE_BANKS - 1:
+                        copied.append((grouped, codes[i], scales[i], g + 1 - QUANTISE_BANKS, t * P))
+                        if len(copied) > 1:
+                            quantise(*copied[-2])
                     if runs_done < len(runs) and runs[runs_done][0] <= banks_done:
                         multiply(*runs[runs_done][1])
                         runs_done += 1
                 j += BANK_TILES
-            next_banks = len(chunks[min(c + 1, len(chunks) - 1)][1]) // BANK_TILES * CHUNK_PASSES
+            next_banks = chunk_tiles[min(c + 1, len(chunks) - 1)] // BANK_TILES * CHUNK_PASSES
             for g in range(0, CHUNK_PASSES, RUN_PASSES):
                 due = banks_done + PASS_LAG + next_banks * (g + RUN_PASSES) // CHUNK_PASSES
                 runs.append((due, (c, codes, scales, g, RUN_PASSES)))
             if s == 0 and c == last_chunk[s]:
                 spread_bias()
 
-        for bank in copied[-QUANTISE_LAG:]:
-            quantise(*bank)
+        quantise(*copied[-1], last=True)
         for due, passes in runs[runs_done:]:
             multiply(*passes)

@@ -27,8 +27,7 @@ TILES_AHEAD = 18
 TRANSPOSE_BANKS = 6
 QUANTISE_BANKS = 2
 PASS_LAG = 4
-VECTOR_COPY_EVERY = 16
-SORT_PERIOD = 3
+SORT_PERIOD = 4
 SORTED_AHEAD = 3
 
 FLOPS = 2 * P * (384 * 12288 + 2 * 512 * 8192 + 2 * 256 * 4096)
@@ -226,10 +225,7 @@ def tile_so2linear_k_kernel(tc, x, W0, b0, W1, W2, out):
                         nc.tensor.transpose(bank[:, b * P : (b + 1) * P], in_words, identity[:])
                     copy_out = grouped[:, g, :].bitcast(F32).rearrange("p (i r u) -> p i r u", i=BANK_TILES, u=HALVES)
                     copy_in = bank[:].rearrange("p (i u r) -> p i r u", i=BANK_TILES, u=HALVES)
-                    if banks_done % VECTOR_COPY_EVERY == VECTOR_COPY_EVERY - 1:
-                        nc.vector.tensor_copy(out=copy_out, in_=copy_in)
-                    else:
-                        nc.scalar.copy(out=copy_out, in_=copy_in)
+                    nc.scalar.copy(out=copy_out, in_=copy_in)
                     banks_done += 1
                     if g % QUANTISE_BANKS == QUANTISE_BANKS - 1:
                         copied.append((grouped, codes[i], scales[i], g + 1 - QUANTISE_BANKS, t * P))

@@ -225,7 +225,10 @@ def tile_so2linear_k_kernel(tc, x, W0, b0, W1, W2, out):
                         nc.tensor.transpose(bank[:, b * P : (b + 1) * P], in_words, identity[:])
                     copy_out = grouped[:, g, :].bitcast(F32).rearrange("p (i r u) -> p i r u", i=BANK_TILES, u=HALVES)
                     copy_in = bank[:].rearrange("p (i u r) -> p i r u", i=BANK_TILES, u=HALVES)
-                    nc.scalar.copy(out=copy_out, in_=copy_in)
+                    if j + BANK_TILES == len(tile_views) and g == 1:
+                        nc.vector.tensor_copy(out=copy_out, in_=copy_in)
+                    else:
+                        nc.scalar.copy(out=copy_out, in_=copy_in)
                     banks_done += 1
                     if g % QUANTISE_BANKS == QUANTISE_BANKS - 1:
                         copied.append((grouped, codes[i], scales[i], g + 1 - QUANTISE_BANKS, t * P))

@@ -72,6 +72,7 @@ def tile_so2linear_k_kernel(tc, x, W0, b0, W1, W2, out):
     first_chunk = [min(c for c, chunk in enumerate(chunks) if chunk[0] == s) for s in range(len(stages))]
     last_chunk = [max(c for c, chunk in enumerate(chunks) if chunk[0] == s) for s in range(len(stages))]
     tile_views = [view for (s, groups) in chunks for group in groups for view in group]
+    last_pair = len(tile_views) - BANK_TILES
     chunk_tiles = [sum(len(group) for group in groups) for (s, groups) in chunks]
 
     with ExitStack() as ctx:
@@ -94,18 +95,14 @@ def tile_so2linear_k_kernel(tc, x, W0, b0, W1, W2, out):
         bias = const.tile([P, 3 * COUT], F32)
         out_sb = const.tile([P, 9 * COUT], F32)
 
-        def load_first_pair():
-            raws = [raw_pool.tile([P, CHUNK_K], BF16, name="raw", tag="raw") for i in range(BANK_TILES)]
-            for g in range(CHUNK_PASSES):
-                k = slice(g * K_PASS, (g + 1) * K_PASS)
-                for raw, view in zip(raws, tile_views):
-                    nc.sync.dma_start(out=raw[:, k], in_=view[:, k])
-            return raws
-
-        def load(j):
-            raw = raw_pool.tile([P, CHUNK_K], BF16, tag="raw")
-            nc.sync.dma_start(out=raw[:], in_=tile_views[j])
-            return raw
+        def load_pair(j):
+            tiles = range(j, j + BANK_TILES)
+            for i in tiles:
+                raw_of[i] = raw_pool.tile([P, CHUNK_K], BF16, name="raw", tag="raw")
+            columns = K_PASS if j in (0, last_pair) else CHUNK_K
+            for k0 in range(0, CHUNK_K, columns):
+                for i in tiles:
+                    nc.sync.dma_start(out=raw_of[i][:, k0 : k0 + columns], in_=tile_views[i][:, k0 : k0 + columns])
 
         def sort_words(raw):
             tile = sorted_pool.tile([P, CHUNK_PASSES, HALVES, P], F32, tag="sorted")
@@ -117,7 +114,7 @@ def tile_so2linear_k_kernel(tc, x, W0, b0, W1, W2, out):
 
         def prepare(j):
             if j < len(tile_views):
-                if j >= chunk_tiles[0] and j % SORT_PERIOD != SORT_PERIOD - 1:
+                if chunk_tiles[0] <= j < last_pair and j % SORT_PERIOD != SORT_PERIOD - 1:
                     halves_of[j] = sort_words(raw_of[j])[:]
                 else:
                     words = raw_of[j][:].bitcast(F32)
@@ -192,9 +189,9 @@ def tile_so2linear_k_kernel(tc, x, W0, b0, W1, W2, out):
                 else:
                     finish_complex(sums_of[s], products[0][2], stages[s]["out_col"])
 
-        raw_of = dict(enumerate(load_first_pair()))
-        for j in range(BANK_TILES, TILES_AHEAD):
-            raw_of[j] = load(j)
+        raw_of = {}
+        for j in range(0, TILES_AHEAD, BANK_TILES):
+            load_pair(j)
 
         for j in range(SORTED_AHEAD):
             prepare(j)
@@ -213,8 +210,8 @@ def tile_so2linear_k_kernel(tc, x, W0, b0, W1, W2, out):
                 scales.append(quantised_pool.tile(shape, U8, name="scales" + tag, tag="scales" + tag, align_bytes=64))
             pairs = [(i, t) for i, group in enumerate(groups) for t in range(0, len(group), BANK_TILES)]
             for i, t in pairs:
-                for tile in range(j + TILES_AHEAD, min(j + TILES_AHEAD + BANK_TILES, len(tile_views))):
-                    raw_of[tile] = load(tile)
+                if j + TILES_AHEAD < len(tile_views):
+                    load_pair(j + TILES_AHEAD)
                 grouped = grouped_pool.tile([P, CHUNK_PASSES, BANK_TILES * K_PASS], BF16, tag="grouped", align_bytes=64)
                 for g in range(CHUNK_PASSES):
                     if g % QUANTISE_BANKS == 0:
@@ -225,7 +222,7 @@ def tile_so2linear_k_kernel(tc, x, W0, b0, W1, W2, out):
                         nc.tensor.transpose(bank[:, b * P : (b + 1) * P], in_words, identity[:])
                     copy_out = grouped[:, g, :].bitcast(F32).rearrange("p (i r u) -> p i r u", i=BANK_TILES, u=HALVES)
                     copy_in = bank[:].rearrange("p (i u r) -> p i r u", i=BANK_TILES, u=HALVES)
-                    if j + BANK_TILES == len(tile_views) and g == 1:
+                    if j == last_pair and g == 1:
                         nc.vector.tensor_copy(out=copy_out, in_=copy_in)
                     else:
                         nc.scalar.copy(out=copy_out, in_=copy_in)

from contextlib import ExitStack

import concourse.masks as masks
import concourse.mybir as mybir

F32 = mybir.dt.float32
BF16 = mybir.dt.bfloat16
U32 = mybir.dt.uint32
U8 = mybir.dt.uint8
FP8X4 = mybir.dt.float8_e4m3fn_x4
ADD = mybir.AluOpType.add
SUBTRACT = mybir.AluOpType.subtract

P = 128
PACK = 4
K_PASS = P * PACK
HALVES = 2
CIN = 4096
COUT = 128
BANK_F32 = 512
BANK_TILES = BANK_F32 // (HALVES * P)

CHUNK_PASSES = 4
CHUNK_K = CHUNK_PASSES * K_PASS
RUN_PASSES = 2
TILES_AHEAD = 18
TRANSPOSE_BANKS = 6
QUANTISE_BANKS = 2
PASS_LAG = 4
SORT_PERIOD = 4
SORTED_AHEAD = 3

FLOPS = 2 * P * (384 * 12288 + 2 * 512 * 8192 + 2 * 256 * 4096)


def list_stages(x_flat, W0, W1, W2):
    def weight_tiles(w, slab):
        return [w[r : r + P, slab * CIN : (slab + 1) * CIN] for r in range(0, w.shape[0], P)]

    def x_tile(component):
        return x_flat[:, component * CIN : (component + 1) * CIN]

    return [
        dict(
            slabs=[[weight_tiles(W1, s), [x_tile(3 + s), x_tile(5 + s)]] for s in range(2)],
            products=[((1, 0), (0, 0), 512), ((1, 1), (0, 0), 512)],
            out_col=3 * COUT,
        ),
        dict(
            slabs=[[weight_tiles(W2, 0), [x_tile(7), x_tile(8)]]],
            products=[((1, 0), (0, 0), 256), ((1, 1), (0, 0), 256)],
            out_col=7 * COUT,
        ),
        dict(
            slabs=[[weight_tiles(W0, s)[:2], weight_tiles(W0, s)[2:] + [x_tile(s)]] for s in range(3)],
            products=[((1, 1), (0, 0), 256), ((1, 1), (1, 0), 128)],
            out_col=0,
        ),
    ]


def tile_so2linear_k_kernel(tc, x, W0, b0, W1, W2, out):
    nc = tc.nc
    out_flat = out.rearrange("e c o -> e (c o)")
    stages = list_stages(x.rearrange("e c k -> e (c k)"), W0, W1, W2)

    chunks = []
    for s, stage in enumerate(stages):
        for slab in stage["slabs"]:
            for k0 in range(0, CIN, CHUNK_K):
                chunks.append((s, [[view[:, k0 : k0 + CHUNK_K] for view in group] for group in slab]))
    first_chunk = [min(c for c, chunk in enumerate(chunks) if chunk[0] == s) for s in range(len(stages))]
    last_chunk = [max(c for c, chunk in enumerate(chunks) if chunk[0] == s) for s in range(len(stages))]
    tile_views = [view for (s, groups) in chunks for group in groups for view in group]
    last_pair = len(tile_views) - BANK_TILES
    chunk_tiles = [sum(len(group) for group in groups) for (s, groups) in chunks]

    with ExitStack() as ctx:
        const = ctx.enter_context(tc.tile_pool(name="const", bufs=1))
        raw_pool = ctx.enter_context(tc.tile_pool(name="raw", bufs=TILES_AHEAD + BANK_TILES))
        sorted_pool = ctx.enter_context(tc.tile_pool(name="sorted", bufs=6))
        grouped_pool = ctx.enter_context(tc.tile_pool(name="grouped", bufs=4))
        quantised_pool = ctx.enter_context(tc.tile_pool(name="quantised", bufs=3))
        bank_pool = ctx.enter_context(tc.psum_pool(name="banks", bufs=TRANSPOSE_BANKS))
        sum_pool = ctx.enter_context(tc.psum_pool(name="sums", bufs=1))
        ctx.enter_context(tc.manual_schedule())

        identity = const.tile([P, P], F32)
        masks.make_identity(nc, identity[:])
        ones = const.tile([P, P], BF16)
        nc.vector.memset(ones[:], 1.0)
        bias_rows = const.tile([P, BANK_F32], BF16)
        nc.vector.memset(bias_rows[:], 0.0)
        nc.scalar.dma_start(out=bias_rows[0:1, 0 : 3 * COUT], in_=b0.rearrange("(o n) -> o n", o=1))
        bias = const.tile([P, 3 * COUT], F32)
        out_sb = const.tile([P, 9 * COUT], F32)

        def load_pair(j):
            tiles = range(j, j + BANK_TILES)
            for i in tiles:
                raw_of[i] = raw_pool.tile([P, CHUNK_K], BF16, name="raw", tag="raw")
            columns = K_PASS if j in (0, last_pair) else CHUNK_K
            for k0 in range(0, CHUNK_K, columns):
                for i in tiles:
                    nc.sync.dma_start(out=raw_of[i][:, k0 : k0 + columns], in_=tile_views[i][:, k0 : k0 + columns])

        def sort_words(raw):
            tile = sorted_pool.tile([P, CHUNK_PASSES, HALVES, P], F32, tag="sorted")
            words = raw[:].bitcast(F32).rearrange("p (g w u) -> p g u w", g=CHUNK_PASSES, u=HALVES)
            nc.vector.tensor_copy(out=tile[:], in_=words)
            return tile

        halves_of = {}

        def prepare(j):
            if j < len(tile_views):
                if chunk_tiles[0] <= j < last_pair and j % SORT_PERIOD != SORT_PERIOD - 1:
                    halves_of[j] = sort_words(raw_of[j])[:]
                else:
                    words = raw_of[j][:].bitcast(F32)
                    halves_of[j] = words.rearrange("p (g w u) -> p g u w", g=CHUNK_PASSES, u=HALVES)

        def quantise(grouped, codes, scales, g, first, last=False):
            columns = BANK_TILES * P
            if codes[:].shape[2] == columns and not last:
                nc.vector.quantize_mx(
                    out=codes[:, g : g + 2, :].rearrange("p g n -> p (g n)").bitcast(FP8X4),
                    scales=scales[:, g : g + 2, :].rearrange("p g n -> p (g n)"),
                    in_=grouped[:, g : g + 2, :].rearrange("p g n -> p (g n)"),
                )
            else:
                for i in range(g, g + 2):
                    nc.vector.quantize_mx(
                        out=codes[:, i, first : first + columns].bitcast(FP8X4),
                        scales=scales[:, i, first : first + columns],
                        in_=grouped[:, i, :],
                    )

        def spread_bias():
            bias_bank = bank_pool.tile([P, BANK_F32], F32, tag="bank")
            nc.tensor.matmul(out=bias_bank[:], lhsT=ones[:], rhs=bias_rows[:], start=True, stop=True)
            nc.scalar.copy(out=bias[:], in_=bias_bank[:, 0 : 3 * COUT])

        def finish_with_bias(sums, col):
            nc.vector.tensor_tensor(out=out_sb[:, col : col + 256], in0=sums[0][:], in1=bias[:, 0:256], op=ADD)
            nc.vector.tensor_tensor(
                out=out_sb[:, col + 256 : col + 384], in0=sums[1][:], in1=bias[:, 256:384], op=ADD
            )
            nc.sync.dma_start(out=out_flat[:, col : col + 384], in_=out_sb[:, col : col + 384])

        def finish_complex(sums, n, col):
            h = n // 2
            from_xr = const.tile([P, n], F32, tag="from_xr")
            nc.scalar.copy(out=from_xr[:], in_=sums[0][:])
            nc.vector.tensor_tensor(
                out=out_sb[:, col : col + h], in0=from_xr[:, 0:h], in1=sums[1][:, h:n], op=SUBTRACT
            )
            nc.vector.tensor_tensor(
                out=out_sb[:, col + h : col + n], in0=from_xr[:, h:n], in1=sums[1][:, 0:h], op=ADD
            )
            nc.sync.dma_start(out=out_flat[:, col : col + n], in_=out_sb[:, col : col + n])

        sums_of = {}

        def multiply(c, codes, scales, g_first, g_count):
            s = chunks[c][0]
            products = stages[s]["products"]
            if c == first_chunk[s] and g_first == 0:
                sums_of[s] = [
                    sum_pool.tile([P, n], F32, name="sum%d" % i, tag="sum%d" % i)
                    for i, (x_tile, w_tile, n) in enumerate(products)
                ]
            for g in range(g_first, g_first + g_count):
                for acc, ((x_group, x_index), (w_group, w_index), n) in zip(sums_of[s], products):
                    x_cols = slice(x_index * P, (x_index + 1) * P)
                    w_cols = slice(w_index * P, w_index * P + n)
                    nc.tensor.matmul_mx(
                        out=acc[:],
                        lhsT=codes[x_group][:, g, x_cols].bitcast(FP8X4),
                        lhsT_scale=scales[x_group][:, g, x_cols],
                        rhs=codes[w_group][:, g, w_cols].bitcast(FP8X4),
                        rhs_scale=scales[w_group][:, g, w_cols],
                        start=(c == first_chunk[s] and g == 0),
                        stop=(c == last_chunk[s] and g == CHUNK_PASSES - 1),
                    )
            if c == last_chunk[s] and g_first + g_count == CHUNK_PASSES:
                if stages[s]["out_col"] == 0:
                    finish_with_bias(sums_of[s], 0)
                else:
                    finish_complex(sums_of[s], products[0][2], stages[s]["out_col"])

        raw_of = {}
        for j in range(0, TILES_AHEAD, BANK_TILES):
            load_pair(j)

        for j in range(SORTED_AHEAD):
            prepare(j)

        j = 0
        banks_done = 0
        copied = []
        runs = []
        runs_done = 0
        for c, (s, groups) in enumerate(chunks):
            codes, scales = [], []
            for i, group in enumerate(groups):
                shape = [P, CHUNK_PASSES, len(group) * P]
                tag = "%d_%d" % (i, len(group))
                codes.append(quantised_pool.tile(shape, U32, name="codes" + tag, tag="codes" + tag, align_bytes=64))
                scales.append(quantised_pool.tile(shape, U8, name="scales" + tag, tag="scales" + tag, align_bytes=64))
            pairs = [(i, t) for i, group in enumerate(groups) for t in range(0, len(group), BANK_TILES)]
            for i, t in pairs:
                if j + TILES_AHEAD < len(tile_views):
                    load_pair(j + TILES_AHEAD)
                grouped = grouped_pool.tile([P, CHUNK_PASSES, BANK_TILES * K_PASS], BF16, tag="grouped", align_bytes=64)
                for g in range(CHUNK_PASSES):
                    if g % QUANTISE_BANKS == 0:
                        prepare(j + SORTED_AHEAD + g // QUANTISE_BANKS)
                    bank = bank_pool.tile([P, BANK_F32], F32, tag="bank")
                    for b in range(BANK_TILES * HALVES):
                        in_words = halves_of[j + b // HALVES][:, g, b % HALVES, :]
                        nc.tensor.transpose(bank[:, b * P : (b + 1) * P], in_words, identity[:])
                    copy_out = grouped[:, g, :].bitcast(F32).rearrange("p (i r u) -> p i r u", i=BANK_TILES, u=HALVES)
                    copy_in = bank[:].rearrange("p (i u r) -> p i r u", i=BANK_TILES, u=HALVES)
                    if j == last_pair and g == 1:
                        nc.vector.tensor_copy(out=copy_out, in_=copy_in)
                    else:
                        nc.scalar.copy(out=copy_out, in_=copy_in)
                    banks_done += 1
                    if g % QUANTISE_BANKS == QUANTISE_BANKS - 1:
                        copied.append((grouped, codes[i], scales[i], g + 1 - QUANTISE_BANKS, t * P))
                        if len(copied) > 1:
                            quantise(*copied[-2])
                    if runs_done < len(runs) and runs[runs_done][0] <= banks_done:
                        multiply(*runs[runs_done][1])
                        runs_done += 1
                j += BANK_TILES
            next_banks = chunk_tiles[min(c + 1, len(chunks) - 1)] // BANK_TILES * CHUNK_PASSES
            for g in range(0, CHUNK_PASSES, RUN_PASSES):
                due = banks_done + PASS_LAG + next_banks * (g + RUN_PASSES) // CHUNK_PASSES
                runs.append((due, (c, codes, scales, g, RUN_PASSES)))
            if s == 0 and c == last_chunk[s]:
                spread_bias()

        quantise(*copied[-1], last=True)
        for due, passes in runs[runs_done:]:
            multiply(*passes)
